import numpy as np
import ml_dtypes


def mxq(x, axis, fmt="e4m3"):
    dtype, down = {"e4m3": (ml_dtypes.float8_e4m3fn, 7), "e5m2": (ml_dtypes.float8_e5m2, 14)}[fmt]
    v = np.moveaxis(np.asarray(x, np.float32).astype(ml_dtypes.bfloat16).astype(np.float64), axis, -1)
    blocks = v.reshape(v.shape[:-1] + (-1, 32))
    amax = np.abs(blocks).max(-1, keepdims=True)
    byte = np.maximum(np.where(amax > 0, np.frexp(amax)[1] - 1 + 127, 0) - down, 1)
    scale = np.exp2(byte - 127.0)
    codes = (blocks / scale).astype(np.float32).astype(dtype).astype(np.float64)
    return np.moveaxis((codes * scale).reshape(v.shape), -1, axis)


WIDE = False


def mx_kscale(k):
    if not WIDE:
        return np.ones(k)
    levels = np.array([10, -10, 5, -5, 0])
    if k % 512:
        return np.exp2(np.random.permutation(np.resize(levels, k // 32))).repeat(32)
    a = np.empty((k // 512, 16))
    for p in range(k // 512):
        a[p, :8] = np.random.permutation(np.resize(levels, 8))
        for g in range(8):
            far = levels[np.abs(levels - a[p, g]) >= 10]
            a[p, g + 8] = far[np.random.randint(len(far))]
    return np.exp2(a.ravel()).repeat(32)


BF16 = ml_dtypes.bfloat16


def bf(x):
    return np.asarray(x, np.float32).astype(BF16)


def f64(x):
    return np.asarray(x).astype(np.float64)


B, S, D, H, QL, KL, ND, VD, RD = 4, 1024, 1024, 4, 512, 512, 64, 128, 64
QH = ND + RD
BASE = 10000.0


def rope(v):
    d = v.shape[-1]
    inv_freq = BASE ** (-np.arange(0, d, 2) / d)
    ang = np.arange(v.shape[1])[:, None] * inv_freq[None, :]
    cos = np.cos(ang)[None, :, None, :]
    sin = np.sin(ang)[None, :, None, :]
    v1 = v[..., 0::2]
    v2 = v[..., 1::2]
    o1 = v1 * cos - v2 * sin
    o2 = v1 * sin + v2 * cos
    return np.stack([o1, o2], axis=-1).reshape(v.shape)


def setup_inputs():
    s, t = mx_kscale(D), mx_kscale(QL)
    return {"x": bf(np.random.standard_normal((B, S, D)) * s),
            "Wqa": bf(np.random.standard_normal((D, QL)) / np.sqrt(D) / s[:, None] * t),
            "Wqb": bf(np.random.standard_normal((QL, H * QH)) / np.sqrt(QL) / t[:, None])}


def reference(x, Wqa, Wqb):
    cq = mxq(f64(x), 2, "e4m3") @ mxq(f64(Wqa), 0, "e4m3")
    q = (mxq(cq, 2, "e4m3") @ mxq(f64(Wqb), 0, "e4m3")).reshape(B, S, H, QH)
    q_nope, q_pe = q[..., :ND], q[..., ND:]
    return np.concatenate([q_nope, rope(q_pe)], axis=-1)

@@ -1,0 +1,273 @@
+import math
+from contextlib import ExitStack
+
+import concourse.masks as masks
+import concourse.mybir as mybir
+
+F32 = mybir.dt.float32
+BF16 = mybir.dt.bfloat16
+I32 = mybir.dt.int32
+U32 = mybir.dt.uint32
+U8 = mybir.dt.uint8
+FP8X4 = mybir.dt.float8_e4m3fn_x4
+ALU = mybir.AluOpType
+SIN = mybir.ActivationFunctionType.Sin
+
+P = 128
+PACK = 4
+K_PASS = P * PACK
+
+TOKENS = 4 * 1024
+SEQ = 1024
+D = 1024
+QL = 512
+HEADS = 4
+HEAD_DIM = 128
+PLAIN = 64
+PAIRS = 32
+BASE = 10000.0
+
+PASSES = D // K_PASS
+WORDS = D // 2
+TILES = 2
+UNIT = TILES * P
+UNITS = TOKENS // UNIT
+TABLES = SEQ // P
+HALF = HEADS * PLAIN
+
+FLOPS = 2 * TOKENS * D * QL + 2 * TOKENS * QL * HEADS * HEAD_DIM
+
+TWO_PI = 2.0 * math.pi
+
+ROUND_FIRST = 2
+ROUND_SECOND = 3
+ROUND_ROTATE = 4
+ROUND_LATE_SETUP = 1
+
+WQA_VECTOR_COLUMNS = 96
+
+
+def rotation_phases(nc, pool, position_int):
+    shape = [P, TABLES, PAIRS, 2]
+    turns = pool.tile(shape, F32)
+    nc.vector.tensor_scalar(
+        out=turns[:, :, 0:1, 1], in0=position_int[:].unsqueeze(2), scalar1=1.0 / TWO_PI, scalar2=None, op0=ALU.mult
+    )
+    for n in (1, 2, 4, 8, 16):
+        nc.vector.tensor_scalar(
+            out=turns[:, :, n : 2 * n, 1],
+            in0=turns[:, :, 0:n, 1],
+            scalar1=BASE ** (-n / PAIRS),
+            scalar2=None,
+            op0=ALU.mult,
+        )
+    nc.vector.tensor_scalar(out=turns[:, :, :, 0], in0=turns[:, :, :, 1], scalar1=0.25, scalar2=None, op0=ALU.add)
+    whole_int = pool.tile(shape, I32)
+    nc.vector.tensor_copy(out=whole_int[:], in_=turns[:])
+    whole = pool.tile(shape, F32)
+    nc.vector.tensor_copy(out=whole[:], in_=whole_int[:])
+    phase = pool.tile(shape, F32)
+    nc.vector.tensor_tensor(out=phase[:], in0=turns[:], in1=whole[:], op=ALU.subtract)
+    return phase
+
+
+def tile_multilatentattention_pa_t_kernel(tc, x, Wqa, Wqb, out):
+    nc = tc.nc
+    x_units = x.flatten_outer_dims().rearrange("(n p t) k -> n p (t k)", p=P, t=TILES)
+    out_units = out.rearrange("b s h d -> (b s) (h d)").rearrange("(n p t) f -> n p t f", p=P, t=TILES)
+
+    with ExitStack() as ctx:
+        keep = ctx.enter_context(tc.tile_pool(name="keep", bufs=1))
+        x_pool = ctx.enter_context(tc.tile_pool(name="x_pool", bufs=UNITS))
+        stage = ctx.enter_context(tc.tile_pool(name="stage", bufs=3))
+        results = ctx.enter_context(tc.tile_pool(name="results", bufs=4))
+        psum = ctx.enter_context(tc.psum_pool(name="psum", bufs=2))
+        ctx.enter_context(tc.manual_schedule())
+
+        wa_raw = keep.tile([P, PASSES, PACK, QL], BF16)
+        nc.sync.dma_start(
+            out=wa_raw[:].rearrange("p g t c -> p g (t c)"),
+            in_=Wqa.rearrange("(g p t) c -> p g (t c)", p=P, t=PACK),
+        )
+        wb_raw = keep.tile([P, PACK, HEADS * HEAD_DIM], BF16)
+        x_tiles = []
+        for n in range(UNITS):
+            x_sb = x_pool.tile([P, TILES * D], BF16)
+            nc.sync.dma_start(out=x_sb[:], in_=x_units[n])
+            x_tiles.append(x_sb)
+            if n == ROUND_FIRST:
+                nc.sync.dma_start(
+                    out=wb_raw[:].rearrange("p j f -> p (j f)"), in_=Wqb.rearrange("(p j) f -> p (j f)", j=PACK)
+                )
+
+        position_int = keep.tile([P, TABLES], I32)
+        nc.gpsimd.iota(
+            position_int[:], pattern=[[UNIT, TABLES // TILES], [1, TILES]], base=0, channel_multiplier=TILES
+        )
+        identity = keep.tile([P, P], F32)
+        masks.make_identity(nc, identity[:])
+        phase = rotation_phases(nc, keep, position_int)
+
+        wa_grouped = keep.tile([P, PASSES, QL * PACK], BF16, align_bytes=64)
+        wa_codes = keep.tile([P, PASSES, QL], U32, align_bytes=64)
+        wa_scales = keep.tile([P, PASSES, QL], U8, align_bytes=64)
+        for g in range(PASSES):
+            wa_sorted = wa_grouped[:, g].rearrange("p (m i t) -> p m i t", m=PACK, t=PACK)
+            wa_rows = wa_raw[:, g].rearrange("p t (i m) -> p m i t", m=PACK)
+            nc.vector.tensor_copy(out=wa_sorted[:, :, 0:WQA_VECTOR_COLUMNS], in_=wa_rows[:, :, 0:WQA_VECTOR_COLUMNS])
+            nc.scalar.copy(out=wa_sorted[:, :, WQA_VECTOR_COLUMNS:P], in_=wa_rows[:, :, WQA_VECTOR_COLUMNS:P])
+        for g in range(PASSES):
+            nc.vector.quantize_mx(out=wa_codes[:, g].bitcast(FP8X4), scales=wa_scales[:, g], in_=wa_grouped[:, g])
+
+        cos_sin = keep.tile([P, TABLES, PAIRS, 2], F32)
+        nc.scalar.activation(out=cos_sin[:], in_=phase[:], func=SIN, scale=TWO_PI)
+        nsin_cos = keep.tile([P, TABLES, PAIRS, 2], F32)
+        wb_codes = keep.tile([P, 2 * HALF], U32, align_bytes=64)
+        wb_scales = keep.tile([P, 2 * HALF], U8, align_bytes=64)
+
+        def late_setup():
+            nc.scalar.mul(out=nsin_cos[:, :, :, 0], in_=cos_sin[:, :, :, 1], mul=-1.0)
+            nc.scalar.copy(out=nsin_cos[:, :, :, 1], in_=cos_sin[:, :, :, 0])
+            wb_grouped = keep.tile([P, 2, HALF * PACK], BF16, align_bytes=64)
+            wb_sorted = wb_raw[:].rearrange("p j (h s f) -> p s h f j", s=2, f=PLAIN)
+            for s in range(2):
+                nc.vector.tensor_copy(
+                    out=wb_grouped[:, s].rearrange("p (h f j) -> p h f j", h=HEADS, j=PACK), in_=wb_sorted[:, s]
+                )
+            nc.vector.quantize_mx(
+                out=wb_codes[:].bitcast(FP8X4), scales=wb_scales[:], in_=wb_grouped[:].rearrange("p s c -> p (s c)")
+            )
+
+        x_grouped, x_packed, cq_grouped, cq_packed = {}, {}, {}, {}
+        plain_banks, rotated_banks, result_tiles = {}, {}, {}
+
+        def transpose_x(n):
+            x_words = x_tiles[n][:].bitcast(F32)
+            grouped = stage.tile([P, PASSES * TILES * P * PACK], BF16, align_bytes=64, name="x_grouped")
+            grouped_words = grouped[:].bitcast(F32).rearrange("p (g t r u) -> p g t r u", g=PASSES, t=TILES, u=2)
+            for t in range(TILES):
+                x_t = psum.tile([P, 2 * PASSES, P], F32, name="x_t")
+                for g in range(PASSES):
+                    first_word = t * WORDS + g * 2 * P
+                    for u in range(2):
+                        every_2nd = x_words[:, first_word + u : first_word + 2 * P : 2]
+                        nc.tensor.transpose(x_t[:, 2 * g + u, :], every_2nd, identity[:])
+                nc.scalar.copy(out=grouped_words[:, :, t], in_=x_t[:].rearrange("p (g u) r -> p g r u", u=2))
+            x_grouped[n] = grouped
+
+        def quantise_x(n):
+            codes = stage.tile([P, PASSES, TILES, P], U32, align_bytes=64, name="x_codes")
+            scales = stage.tile([P, PASSES, TILES, P], U8, align_bytes=64, name="x_scales")
+            nc.vector.quantize_mx(
+                out=codes[:].rearrange("p g t r -> p (g t r)").bitcast(FP8X4),
+                scales=scales[:].rearrange("p g t r -> p (g t r)"),
+                in_=x_grouped[n][:],
+            )
+            x_packed[n] = (codes, scales)
+
+        def first_product(n):
+            codes, scales = x_packed[n]
+            grouped = stage.tile([P, TILES, P, PACK], BF16, align_bytes=64, name="cq_grouped")
+            for t in range(TILES):
+                cq_t = psum.tile([P, PACK, P], F32, name="cq_t")
+                for m in range(PACK):
+                    columns = slice(m * P, (m + 1) * P)
+                    for g in range(PASSES):
+                        nc.tensor.matmul_mx(
+                            out=cq_t[:, m, :],
+                            lhsT=wa_codes[:, g, columns].bitcast(FP8X4),
+                            lhsT_scale=wa_scales[:, g, columns],
+                            rhs=codes[:, g, t, :].bitcast(FP8X4),
+                            rhs_scale=scales[:, g, t, :],
+                            start=(g == 0),
+                            stop=(g == PASSES - 1),
+                        )
+                nc.scalar.copy(out=grouped[:, t], in_=cq_t[:].rearrange("p m r -> p r m"))
+            cq_grouped[n] = grouped
+
+        def quantise_cq(n):
+            codes = stage.tile([P, TILES, P], U32, align_bytes=64, name="cq_codes")
+            scales = stage.tile([P, TILES, P], U8, align_bytes=64, name="cq_scales")
+            nc.vector.quantize_mx(
+                out=codes[:].rearrange("p t r -> p (t r)").bitcast(FP8X4),
+                scales=scales[:].rearrange("p t r -> p (t r)"),
+                in_=cq_grouped[n][:].rearrange("p t r m -> p (t r m)"),
+            )
+            cq_packed[n] = (codes, scales)
+
+        def second_product(n):
+            codes, scales = cq_packed[n]
+            plain_bank = psum.tile([P, TILES, HALF], F32, name="plain_bank")
+            rotated_bank = psum.tile([P, TILES, HALF], F32, name="rotated_bank")
+            for t in range(TILES):
+                for s, bank in enumerate((plain_bank, rotated_bank)):
+                    columns = slice(s * HALF, (s + 1) * HALF)
+                    nc.tensor.matmul_mx(
+                        out=bank[:, t, :],
+                        lhsT=codes[:, t, :].bitcast(FP8X4),
+                        lhsT_scale=scales[:, t, :],
+                        rhs=wb_codes[:, columns].bitcast(FP8X4),
+                        rhs_scale=wb_scales[:, columns],
+                        start=True,
+                        stop=True,
+                    )
+            plain_banks[n] = plain_bank
+            rotated_banks[n] = rotated_bank
+            result_tiles[n] = results.tile([P, TILES, HEADS, HEAD_DIM], F32, name="result")
+
+        def copy_plain(n, engine_copy):
+            engine_copy(
+                out=result_tiles[n][:, :, :, 0:PLAIN], in_=plain_banks[n][:].rearrange("p t (h f) -> p t h f", f=PLAIN)
+            )
+
+        def rotate_and_store(n):
+            step = TILES if n < UNITS - 1 else 1
+            first_table = (n % (TABLES // TILES)) * TILES
+            pairs = rotated_banks[n][:].rearrange("p t (h j e) -> p t h j e", h=HEADS, e=2)
+            result = result_tiles[n]
+            from_w = stage.tile([P, TILES, HEADS, PAIRS, 2], F32, name="from_w")
+            for t in range(0, TILES, step):
+                shape = [P, step, HEADS, PAIRS, 2]
+                tiles = slice(t, t + step)
+                tables = slice(first_table + t, first_table + t + step)
+                rotated = result[:, tiles, :, PLAIN:HEAD_DIM].rearrange("p t h (j e) -> p t h j e", e=2)
+                nc.vector.tensor_tensor(
+                    out=rotated,
+                    in0=pairs[:, tiles, :, :, 0:1].to_broadcast(shape),
+                    in1=cos_sin[:, tables].unsqueeze(2).to_broadcast(shape),
+                    op=ALU.mult,
+                )
+                nc.vector.tensor_tensor(
+                    out=from_w[:, tiles],
+                    in0=pairs[:, tiles, :, :, 1:2].to_broadcast(shape),
+                    in1=nsin_cos[:, tables].unsqueeze(2).to_broadcast(shape),
+                    op=ALU.mult,
+                )
+                nc.gpsimd.tensor_tensor(out=rotated, in0=rotated, in1=from_w[:, tiles], op=ALU.add)
+                nc.sync.dma_start(out=out_units[n][:, tiles], in_=result[:, tiles].rearrange("p t h d -> p t (h d)"))
+
+        def vector_copies_plain(n):
+            return n % 2 == 1 and n + ROUND_ROTATE < UNITS
+
+        def in_range(n):
+            return 0 <= n < UNITS
+
+        for i in range(UNITS + ROUND_ROTATE):
+            if in_range(i):
+                transpose_x(i)
+            if in_range(i - ROUND_FIRST):
+                first_product(i - ROUND_FIRST)
+            if in_range(i - ROUND_SECOND):
+                second_product(i - ROUND_SECOND)
+                if not vector_copies_plain(i - ROUND_SECOND):
+                    copy_plain(i - ROUND_SECOND, nc.scalar.copy)
+            if in_range(i - ROUND_ROTATE):
+                if vector_copies_plain(i - ROUND_ROTATE):
+                    copy_plain(i - ROUND_ROTATE, nc.vector.tensor_copy)
+                rotate_and_store(i - ROUND_ROTATE)
+            if in_range(i):
+                quantise_x(i)
+            if in_range(i - ROUND_FIRST):
+                quantise_cq(i - ROUND_FIRST)
+            if i == ROUND_LATE_SETUP:
+                late_setup()

@@ -39,10 +39,11 @@ FLOPS = 2 * TOKENS * D * QL + 2 * TOKENS * QL * HEADS * HEAD_DIM
 
 TWO_PI = 2.0 * math.pi
 
-ROUND_FIRST = 2
-ROUND_SECOND = 3
-ROUND_ROTATE = 4
-ROUND_LATE_SETUP = 1
+ROUND_FIRST = 4
+ROUND_SECOND = 5
+ROUND_ROTATE = 6
+ROUND_SETUP_A = 1
+ROUND_SETUP_B = 3
 
 WQA_VECTOR_COLUMNS = 96
 
@@ -79,53 +80,65 @@ def tile_multilatentattention_pa_t_kernel(tc, x, Wqa, Wqb, out):
     with ExitStack() as ctx:
         keep = ctx.enter_context(tc.tile_pool(name="keep", bufs=1))
         x_pool = ctx.enter_context(tc.tile_pool(name="x_pool", bufs=UNITS))
+        x_stage = ctx.enter_context(tc.tile_pool(name="x_stage", bufs=ROUND_FIRST + 2))
         stage = ctx.enter_context(tc.tile_pool(name="stage", bufs=3))
         results = ctx.enter_context(tc.tile_pool(name="results", bufs=4))
         psum = ctx.enter_context(tc.psum_pool(name="psum", bufs=2))
         ctx.enter_context(tc.manual_schedule())
 
         wa_raw = keep.tile([P, PASSES, PACK, QL], BF16)
-        nc.sync.dma_start(
-            out=wa_raw[:].rearrange("p g t c -> p g (t c)"),
-            in_=Wqa.rearrange("(g p t) c -> p g (t c)", p=P, t=PACK),
-        )
         wb_raw = keep.tile([P, PACK, HEADS * HEAD_DIM], BF16)
         x_tiles = []
         for n in range(UNITS):
             x_sb = x_pool.tile([P, TILES * D], BF16)
-            nc.sync.dma_start(out=x_sb[:], in_=x_units[n])
+            if n == 0:
+                for t in range(TILES):
+                    columns = slice(t * D, (t + 1) * D)
+                    nc.sync.dma_start(out=x_sb[:, columns], in_=x_units[n][:, columns])
+            else:
+                nc.sync.dma_start(out=x_sb[:], in_=x_units[n])
             x_tiles.append(x_sb)
-            if n == ROUND_FIRST:
+            if n == ROUND_SETUP_A:
+                nc.sync.dma_start(
+                    out=wa_raw[:].rearrange("p g t c -> p g (t c)"),
+                    in_=Wqa.rearrange("(g p t) c -> p g (t c)", p=P, t=PACK),
+                )
+            if n == ROUND_SETUP_B:
                 nc.sync.dma_start(
                     out=wb_raw[:].rearrange("p j f -> p (j f)"), in_=Wqb.rearrange("(p j) f -> p (j f)", j=PACK)
                 )
 
+        identity = keep.tile([P, P], F32)
+        masks.make_identity(nc, identity[:])
         position_int = keep.tile([P, TABLES], I32)
         nc.gpsimd.iota(
             position_int[:], pattern=[[UNIT, TABLES // TILES], [1, TILES]], base=0, channel_multiplier=TILES
         )
-        identity = keep.tile([P, P], F32)
-        masks.make_identity(nc, identity[:])
         phase = rotation_phases(nc, keep, position_int)
 
-        wa_grouped = keep.tile([P, PASSES, QL * PACK], BF16, align_bytes=64)
+        first_sine = keep.tile([P, 1], F32)
+        nc.scalar.activation(out=first_sine[:], in_=identity[:, 0:1], func=SIN)
+        cos_sin = keep.tile([P, TABLES, PAIRS, 2], F32)
+        nsin_cos = keep.tile([P, TABLES, PAIRS, 2], F32)
         wa_codes = keep.tile([P, PASSES, QL], U32, align_bytes=64)
         wa_scales = keep.tile([P, PASSES, QL], U8, align_bytes=64)
-        for g in range(PASSES):
-            wa_sorted = wa_grouped[:, g].rearrange("p (m i t) -> p m i t", m=PACK, t=PACK)
-            wa_rows = wa_raw[:, g].rearrange("p t (i m) -> p m i t", m=PACK)
-            nc.vector.tensor_copy(out=wa_sorted[:, :, 0:WQA_VECTOR_COLUMNS], in_=wa_rows[:, :, 0:WQA_VECTOR_COLUMNS])
-            nc.scalar.copy(out=wa_sorted[:, :, WQA_VECTOR_COLUMNS:P], in_=wa_rows[:, :, WQA_VECTOR_COLUMNS:P])
-        for g in range(PASSES):
-            nc.vector.quantize_mx(out=wa_codes[:, g].bitcast(FP8X4), scales=wa_scales[:, g], in_=wa_grouped[:, g])
-
-        cos_sin = keep.tile([P, TABLES, PAIRS, 2], F32)
-        nc.scalar.activation(out=cos_sin[:], in_=phase[:], func=SIN, scale=TWO_PI)
-        nsin_cos = keep.tile([P, TABLES, PAIRS, 2], F32)
         wb_codes = keep.tile([P, 2 * HALF], U32, align_bytes=64)
         wb_scales = keep.tile([P, 2 * HALF], U8, align_bytes=64)
 
-        def late_setup():
+        def setup_a():
+            wa_grouped = keep.tile([P, PASSES, QL * PACK], BF16, align_bytes=64)
+            for g in range(PASSES):
+                wa_sorted = wa_grouped[:, g].rearrange("p (m i t) -> p m i t", m=PACK, t=PACK)
+                wa_rows = wa_raw[:, g].rearrange("p t (i m) -> p m i t", m=PACK)
+                nc.vector.tensor_copy(
+                    out=wa_sorted[:, :, 0:WQA_VECTOR_COLUMNS], in_=wa_rows[:, :, 0:WQA_VECTOR_COLUMNS]
+                )
+                nc.scalar.copy(out=wa_sorted[:, :, WQA_VECTOR_COLUMNS:P], in_=wa_rows[:, :, WQA_VECTOR_COLUMNS:P])
+            for g in range(PASSES):
+                nc.vector.quantize_mx(out=wa_codes[:, g].bitcast(FP8X4), scales=wa_scales[:, g], in_=wa_grouped[:, g])
+
+        def setup_b():
+            nc.scalar.activation(out=cos_sin[:], in_=phase[:], func=SIN, scale=TWO_PI)
             nc.scalar.mul(out=nsin_cos[:, :, :, 0], in_=cos_sin[:, :, :, 1], mul=-1.0)
             nc.scalar.copy(out=nsin_cos[:, :, :, 1], in_=cos_sin[:, :, :, 0])
             wb_grouped = keep.tile([P, 2, HALF * PACK], BF16, align_bytes=64)
@@ -143,7 +156,7 @@ def tile_multilatentattention_pa_t_kernel(tc, x, Wqa, Wqb, out):
 
         def transpose_x(n):
             x_words = x_tiles[n][:].bitcast(F32)
-            grouped = stage.tile([P, PASSES * TILES * P * PACK], BF16, align_bytes=64, name="x_grouped")
+            grouped = x_stage.tile([P, PASSES * TILES * P * PACK], BF16, align_bytes=64, name="x_grouped")
             grouped_words = grouped[:].bitcast(F32).rearrange("p (g t r u) -> p g t r u", g=PASSES, t=TILES, u=2)
             for t in range(TILES):
                 x_t = psum.tile([P, 2 * PASSES, P], F32, name="x_t")
@@ -156,14 +169,19 @@ def tile_multilatentattention_pa_t_kernel(tc, x, Wqa, Wqb, out):
             x_grouped[n] = grouped
 
         def quantise_x(n):
-            codes = stage.tile([P, PASSES, TILES, P], U32, align_bytes=64, name="x_codes")
-            scales = stage.tile([P, PASSES, TILES, P], U8, align_bytes=64, name="x_scales")
+            codes = x_stage.tile([P, PASSES, TILES, P], U32, align_bytes=64, name="x_codes")
+            scales = x_stage.tile([P, PASSES, TILES, P], U8, align_bytes=64, name="x_scales")
             nc.vector.quantize_mx(
                 out=codes[:].rearrange("p g t r -> p (g t r)").bitcast(FP8X4),
                 scales=scales[:].rearrange("p g t r -> p (g t r)"),
                 in_=x_grouped[n][:],
             )
             x_packed[n] = (codes, scales)
+
+        def steps(n):
+            if n < UNITS - 1:
+                return [slice(0, TILES)]
+            return [slice(t, t + 1) for t in range(TILES)]
 
         def first_product(n):
             codes, scales = x_packed[n]
@@ -188,48 +206,57 @@ def tile_multilatentattention_pa_t_kernel(tc, x, Wqa, Wqb, out):
         def quantise_cq(n):
             codes = stage.tile([P, TILES, P], U32, align_bytes=64, name="cq_codes")
             scales = stage.tile([P, TILES, P], U8, align_bytes=64, name="cq_scales")
-            nc.vector.quantize_mx(
-                out=codes[:].rearrange("p t r -> p (t r)").bitcast(FP8X4),
-                scales=scales[:].rearrange("p t r -> p (t r)"),
-                in_=cq_grouped[n][:].rearrange("p t r m -> p (t r m)"),
-            )
+            for tiles in steps(n):
+                nc.vector.quantize_mx(
+                    out=codes[:, tiles].rearrange("p t r -> p (t r)").bitcast(FP8X4),
+                    scales=scales[:, tiles].rearrange("p t r -> p (t r)"),
+                    in_=cq_grouped[n][:, tiles].rearrange("p t r m -> p (t r m)"),
+                )
             cq_packed[n] = (codes, scales)
 
         def second_product(n):
             codes, scales = cq_packed[n]
-            plain_bank = psum.tile([P, TILES, HALF], F32, name="plain_bank")
-            rotated_bank = psum.tile([P, TILES, HALF], F32, name="rotated_bank")
-            for t in range(TILES):
-                for s, bank in enumerate((plain_bank, rotated_bank)):
-                    columns = slice(s * HALF, (s + 1) * HALF)
-                    nc.tensor.matmul_mx(
-                        out=bank[:, t, :],
-                        lhsT=codes[:, t, :].bitcast(FP8X4),
-                        lhsT_scale=scales[:, t, :],
-                        rhs=wb_codes[:, columns].bitcast(FP8X4),
-                        rhs_scale=wb_scales[:, columns],
-                        start=True,
-                        stop=True,
-                    )
-            plain_banks[n] = plain_bank
-            rotated_banks[n] = rotated_bank
-            result_tiles[n] = results.tile([P, TILES, HEADS, HEAD_DIM], F32, name="result")
+            result = results.tile([P, TILES, HEADS, HEAD_DIM], F32, name="result")
+            for tiles in steps(n):
+                if tiles.start == 0:
+                    plain_bank = psum.tile([P, TILES, HALF], F32, name="plain_bank")
+                    rotated_bank = psum.tile([P, TILES, HALF], F32, name="rotated_bank")
+                else:
+                    plain_bank = psum.tile([P, TILES, HALF], F32, name="x_t")
+                    rotated_bank = psum.tile([P, TILES, HALF], F32, name="x_t")
+                for t in range(tiles.start, tiles.stop):
+                    for s, bank in enumerate((plain_bank, rotated_bank)):
+                        columns = slice(s * HALF, (s + 1) * HALF)
+                        nc.tensor.matmul_mx(
+                            out=bank[:, t, :],
+                            lhsT=codes[:, t, :].bitcast(FP8X4),
+                            lhsT_scale=scales[:, t, :],
+                            rhs=wb_codes[:, columns].bitcast(FP8X4),
+                            rhs_scale=wb_scales[:, columns],
+                            start=True,
+                            stop=True,
+                        )
+                plain_banks[n, tiles.start] = plain_bank
+                rotated_banks[n, tiles.start] = rotated_bank
+            result_tiles[n] = result
 
         def copy_plain(n, engine_copy):
-            engine_copy(
-                out=result_tiles[n][:, :, :, 0:PLAIN], in_=plain_banks[n][:].rearrange("p t (h f) -> p t h f", f=PLAIN)
-            )
+            for tiles in steps(n):
+                engine_copy(
+                    out=result_tiles[n][:, tiles, :, 0:PLAIN],
+                    in_=plain_banks[n, tiles.start][:, tiles].rearrange("p t (h f) -> p t h f", f=PLAIN),
+                )
 
         def rotate_and_store(n):
-            step = TILES if n < UNITS - 1 else 1
             first_table = (n % (TABLES // TILES)) * TILES
-            pairs = rotated_banks[n][:].rearrange("p t (h j e) -> p t h j e", h=HEADS, e=2)
             result = result_tiles[n]
             from_w = stage.tile([P, TILES, HEADS, PAIRS, 2], F32, name="from_w")
-            for t in range(0, TILES, step):
-                shape = [P, step, HEADS, PAIRS, 2]
-                tiles = slice(t, t + step)
-                tables = slice(first_table + t, first_table + t + step)
+            rotated_views = []
+            add_engine = nc.gpsimd if n < UNITS - 1 else nc.vector
+            for tiles in steps(n):
+                pairs = rotated_banks[n, tiles.start][:].rearrange("p t (h j e) -> p t h j e", h=HEADS, e=2)
+                shape = [P, tiles.stop - tiles.start, HEADS, PAIRS, 2]
+                tables = slice(first_table + tiles.start, first_table + tiles.stop)
                 rotated = result[:, tiles, :, PLAIN:HEAD_DIM].rearrange("p t h (j e) -> p t h j e", e=2)
                 nc.vector.tensor_tensor(
                     out=rotated,
@@ -243,7 +270,9 @@ def tile_multilatentattention_pa_t_kernel(tc, x, Wqa, Wqb, out):
                     in1=nsin_cos[:, tables].unsqueeze(2).to_broadcast(shape),
                     op=ALU.mult,
                 )
-                nc.gpsimd.tensor_tensor(out=rotated, in0=rotated, in1=from_w[:, tiles], op=ALU.add)
+                rotated_views.append(rotated)
+            for tiles, rotated in zip(steps(n), rotated_views):
+                add_engine.tensor_tensor(out=rotated, in0=rotated, in1=from_w[:, tiles], op=ALU.add)
                 nc.sync.dma_start(out=out_units[n][:, tiles], in_=result[:, tiles].rearrange("p t h d -> p t (h d)"))
 
         def vector_copies_plain(n):
@@ -269,5 +298,7 @@ def tile_multilatentattention_pa_t_kernel(tc, x, Wqa, Wqb, out):
                 quantise_x(i)
             if in_range(i - ROUND_FIRST):
                 quantise_cq(i - ROUND_FIRST)
-            if i == ROUND_LATE_SETUP:
-                late_setup()
+            if i == ROUND_SETUP_A:
+                setup_a()
+            if i == ROUND_SETUP_B:
+                setup_b()

@@ -151,11 +151,23 @@ def tile_multilatentattention_pa_t_kernel(tc, x, Wqa, Wqb, out):
                 out=wb_codes[:].bitcast(FP8X4), scales=wb_scales[:], in_=wb_grouped[:].rearrange("p s c -> p (s c)")
             )
 
-        x_grouped, x_packed, cq_grouped, cq_packed = {}, {}, {}, {}
+        x_splits, x_grouped, x_packed, cq_grouped, cq_packed = {}, {}, {}, {}, {}
         plain_banks, rotated_banks, result_tiles = {}, {}, {}
 
+        def split_x(n):
+            split = x_stage.tile([P, TILES * D], BF16, align_bytes=64, name="x_split")
+            nc.vector.tensor_copy(
+                out=split[:].bitcast(F32).rearrange("p (a u i) -> p a u i", u=2, i=P),
+                in_=x_tiles[n][:].bitcast(F32).rearrange("p (a i u) -> p a u i", u=2, i=P),
+            )
+            x_splits[n] = split
+
+        def word_columns(n, first_word, u):
+            if n in x_splits:
+                return x_splits[n][:].bitcast(F32)[:, first_word + u * P : first_word + (u + 1) * P]
+            return x_tiles[n][:].bitcast(F32)[:, first_word + u : first_word + 2 * P : 2]
+
         def transpose_x(n):
-            x_words = x_tiles[n][:].bitcast(F32)
             grouped = x_stage.tile([P, PASSES * TILES * P * PACK], BF16, align_bytes=64, name="x_grouped")
             grouped_words = grouped[:].bitcast(F32).rearrange("p (g t r u) -> p g t r u", g=PASSES, t=TILES, u=2)
             for t in range(TILES):
@@ -163,8 +175,7 @@ def tile_multilatentattention_pa_t_kernel(tc, x, Wqa, Wqb, out):
                 for g in range(PASSES):
                     first_word = t * WORDS + g * 2 * P
                     for u in range(2):
-                        every_2nd = x_words[:, first_word + u : first_word + 2 * P : 2]
-                        nc.tensor.transpose(x_t[:, 2 * g + u, :], every_2nd, identity[:])
+                        nc.tensor.transpose(x_t[:, 2 * g + u, :], word_columns(n, first_word, u), identity[:])
                 nc.scalar.copy(out=grouped_words[:, :, t], in_=x_t[:].rearrange("p (g u) r -> p g r u", u=2))
             x_grouped[n] = grouped
 
@@ -276,7 +287,7 @@ def tile_multilatentattention_pa_t_kernel(tc, x, Wqa, Wqb, out):
                 nc.sync.dma_start(out=out_units[n][:, tiles], in_=result[:, tiles].rearrange("p t h d -> p t (h d)"))
 
         def vector_copies_plain(n):
-            return n % 2 == 1 and n + ROUND_ROTATE < UNITS
+            return False
 
         def in_range(n):
             return 0 <= n < UNITS
@@ -302,3 +313,5 @@ def tile_multilatentattention_pa_t_kernel(tc, x, Wqa, Wqb, out):
                 setup_a()
             if i == ROUND_SETUP_B:
                 setup_b()
+            if i >= ROUND_SETUP_B and in_range(i + 2):
+                split_x(i + 2)

@@ -44,6 +44,7 @@ ROUND_SECOND = 5
 ROUND_ROTATE = 6
 ROUND_SETUP_A = 1
 ROUND_SETUP_B = 3
+SPLIT_AHEAD = 3
 
 WQA_VECTOR_COLUMNS = 96
 
@@ -81,6 +82,7 @@ def tile_multilatentattention_pa_t_kernel(tc, x, Wqa, Wqb, out):
         keep = ctx.enter_context(tc.tile_pool(name="keep", bufs=1))
         x_pool = ctx.enter_context(tc.tile_pool(name="x_pool", bufs=UNITS))
         x_stage = ctx.enter_context(tc.tile_pool(name="x_stage", bufs=ROUND_FIRST + 2))
+        x_splits_pool = ctx.enter_context(tc.tile_pool(name="x_splits_pool", bufs=8))
         stage = ctx.enter_context(tc.tile_pool(name="stage", bufs=3))
         results = ctx.enter_context(tc.tile_pool(name="results", bufs=4))
         psum = ctx.enter_context(tc.psum_pool(name="psum", bufs=2))
@@ -99,10 +101,9 @@ def tile_multilatentattention_pa_t_kernel(tc, x, Wqa, Wqb, out):
                 nc.sync.dma_start(out=x_sb[:], in_=x_units[n])
             x_tiles.append(x_sb)
             if n == ROUND_SETUP_A:
-                nc.sync.dma_start(
-                    out=wa_raw[:].rearrange("p g t c -> p g (t c)"),
-                    in_=Wqa.rearrange("(g p t) c -> p g (t c)", p=P, t=PACK),
-                )
+                wa_passes = Wqa.rearrange("(g p t) c -> g p (t c)", p=P, t=PACK)
+                for g in range(PASSES):
+                    nc.sync.dma_start(out=wa_raw[:, g].rearrange("p t c -> p (t c)"), in_=wa_passes[g])
             if n == ROUND_SETUP_B:
                 nc.sync.dma_start(
                     out=wb_raw[:].rearrange("p j f -> p (j f)"), in_=Wqb.rearrange("(p j) f -> p (j f)", j=PACK)
@@ -115,7 +116,6 @@ def tile_multilatentattention_pa_t_kernel(tc, x, Wqa, Wqb, out):
             position_int[:], pattern=[[UNIT, TABLES // TILES], [1, TILES]], base=0, channel_multiplier=TILES
         )
         phase = rotation_phases(nc, keep, position_int)
-
         first_sine = keep.tile([P, 1], F32)
         nc.scalar.activation(out=first_sine[:], in_=identity[:, 0:1], func=SIN)
         cos_sin = keep.tile([P, TABLES, PAIRS, 2], F32)
@@ -126,6 +126,16 @@ def tile_multilatentattention_pa_t_kernel(tc, x, Wqa, Wqb, out):
         wb_scales = keep.tile([P, 2 * HALF], U8, align_bytes=64)
 
         def setup_a():
+            nc.scalar.activation(out=cos_sin[:], in_=phase[:], func=SIN, scale=TWO_PI)
+            for e, sign in enumerate((-1.0, 1.0)):
+                nc.gpsimd.tensor_scalar(
+                    out=nsin_cos[:, :, :, e],
+                    in0=cos_sin[:, :, :, 1 - e],
+                    scalar1=sign,
+                    scalar2=0.0,
+                    op0=ALU.mult,
+                    op1=ALU.add,
+                )
             wa_grouped = keep.tile([P, PASSES, QL * PACK], BF16, align_bytes=64)
             for g in range(PASSES):
                 wa_sorted = wa_grouped[:, g].rearrange("p (m i t) -> p m i t", m=PACK, t=PACK)
@@ -138,9 +148,6 @@ def tile_multilatentattention_pa_t_kernel(tc, x, Wqa, Wqb, out):
                 nc.vector.quantize_mx(out=wa_codes[:, g].bitcast(FP8X4), scales=wa_scales[:, g], in_=wa_grouped[:, g])
 
         def setup_b():
-            nc.scalar.activation(out=cos_sin[:], in_=phase[:], func=SIN, scale=TWO_PI)
-            nc.scalar.mul(out=nsin_cos[:, :, :, 0], in_=cos_sin[:, :, :, 1], mul=-1.0)
-            nc.scalar.copy(out=nsin_cos[:, :, :, 1], in_=cos_sin[:, :, :, 0])
             wb_grouped = keep.tile([P, 2, HALF * PACK], BF16, align_bytes=64)
             wb_sorted = wb_raw[:].rearrange("p j (h s f) -> p s h f j", s=2, f=PLAIN)
             for s in range(2):
@@ -151,12 +158,12 @@ def tile_multilatentattention_pa_t_kernel(tc, x, Wqa, Wqb, out):
                 out=wb_codes[:].bitcast(FP8X4), scales=wb_scales[:], in_=wb_grouped[:].rearrange("p s c -> p (s c)")
             )
 
-        x_splits, x_grouped, x_packed, cq_grouped, cq_packed = {}, {}, {}, {}, {}
-        plain_banks, rotated_banks, result_tiles = {}, {}, {}
+        x_splits, x_packed, cq_grouped, cq_packed = {}, {}, {}, {}
+        plain_banks, rotated_banks, result_tiles, from_w_tiles = {}, {}, {}, {}
 
         def split_x(n):
-            split = x_stage.tile([P, TILES * D], BF16, align_bytes=64, name="x_split")
-            nc.vector.tensor_copy(
+            split = x_splits_pool.tile([P, TILES * D], BF16, align_bytes=64, name="x_split")
+            nc.gpsimd.tensor_copy(
                 out=split[:].bitcast(F32).rearrange("p (a u i) -> p a u i", u=2, i=P),
                 in_=x_tiles[n][:].bitcast(F32).rearrange("p (a i u) -> p a u i", u=2, i=P),
             )
@@ -166,6 +173,8 @@ def tile_multilatentattention_pa_t_kernel(tc, x, Wqa, Wqb, out):
             if n in x_splits:
                 return x_splits[n][:].bitcast(F32)[:, first_word + u * P : first_word + (u + 1) * P]
             return x_tiles[n][:].bitcast(F32)[:, first_word + u : first_word + 2 * P : 2]
+
+        x_grouped = {}
 
         def transpose_x(n):
             grouped = x_stage.tile([P, PASSES * TILES * P * PACK], BF16, align_bytes=64, name="x_grouped")
@@ -189,15 +198,12 @@ def tile_multilatentattention_pa_t_kernel(tc, x, Wqa, Wqb, out):
             )
             x_packed[n] = (codes, scales)
 
-        def steps(n):
-            if n < UNITS - 1:
-                return [slice(0, TILES)]
-            return [slice(t, t + 1) for t in range(TILES)]
-
-        def first_product(n):
+        def first_product(n, tiles):
+            if n not in cq_grouped:
+                grouped = stage.tile([P, TILES, P, PACK], BF16, align_bytes=64, name="cq_grouped")
+                cq_grouped[n] = grouped
             codes, scales = x_packed[n]
-            grouped = stage.tile([P, TILES, P, PACK], BF16, align_bytes=64, name="cq_grouped")
-            for t in range(TILES):
+            for t in tiles:
                 cq_t = psum.tile([P, PACK, P], F32, name="cq_t")
                 for m in range(PACK):
                     columns = slice(m * P, (m + 1) * P)
@@ -211,107 +217,136 @@ def tile_multilatentattention_pa_t_kernel(tc, x, Wqa, Wqb, out):
                             start=(g == 0),
                             stop=(g == PASSES - 1),
                         )
-                nc.scalar.copy(out=grouped[:, t], in_=cq_t[:].rearrange("p m r -> p r m"))
-            cq_grouped[n] = grouped
+                nc.scalar.copy(out=cq_grouped[n][:, t], in_=cq_t[:].rearrange("p m r -> p r m"))
 
-        def quantise_cq(n):
-            codes = stage.tile([P, TILES, P], U32, align_bytes=64, name="cq_codes")
-            scales = stage.tile([P, TILES, P], U8, align_bytes=64, name="cq_scales")
-            for tiles in steps(n):
-                nc.vector.quantize_mx(
-                    out=codes[:, tiles].rearrange("p t r -> p (t r)").bitcast(FP8X4),
-                    scales=scales[:, tiles].rearrange("p t r -> p (t r)"),
-                    in_=cq_grouped[n][:, tiles].rearrange("p t r m -> p (t r m)"),
-                )
-            cq_packed[n] = (codes, scales)
-
-        def second_product(n):
+        def quantise_cq(n, tiles):
+            if n not in cq_packed:
+                codes = stage.tile([P, TILES, P], U32, align_bytes=64, name="cq_codes")
+                scales = stage.tile([P, TILES, P], U8, align_bytes=64, name="cq_scales")
+                cq_packed[n] = (codes, scales)
             codes, scales = cq_packed[n]
-            result = results.tile([P, TILES, HEADS, HEAD_DIM], F32, name="result")
-            for tiles in steps(n):
-                if tiles.start == 0:
-                    plain_bank = psum.tile([P, TILES, HALF], F32, name="plain_bank")
-                    rotated_bank = psum.tile([P, TILES, HALF], F32, name="rotated_bank")
-                else:
-                    plain_bank = psum.tile([P, TILES, HALF], F32, name="x_t")
-                    rotated_bank = psum.tile([P, TILES, HALF], F32, name="x_t")
-                for t in range(tiles.start, tiles.stop):
-                    for s, bank in enumerate((plain_bank, rotated_bank)):
-                        columns = slice(s * HALF, (s + 1) * HALF)
-                        nc.tensor.matmul_mx(
-                            out=bank[:, t, :],
-                            lhsT=codes[:, t, :].bitcast(FP8X4),
-                            lhsT_scale=scales[:, t, :],
-                            rhs=wb_codes[:, columns].bitcast(FP8X4),
-                            rhs_scale=wb_scales[:, columns],
-                            start=True,
-                            stop=True,
-                        )
-                plain_banks[n, tiles.start] = plain_bank
-                rotated_banks[n, tiles.start] = rotated_bank
-            result_tiles[n] = result
+            part = slice(tiles[0], tiles[-1] + 1)
+            nc.vector.quantize_mx(
+                out=codes[:, part].rearrange("p t r -> p (t r)").bitcast(FP8X4),
+                scales=scales[:, part].rearrange("p t r -> p (t r)"),
+                in_=cq_grouped[n][:, part].rearrange("p t r m -> p (t r m)"),
+            )
 
-        def copy_plain(n, engine_copy):
-            for tiles in steps(n):
-                engine_copy(
-                    out=result_tiles[n][:, tiles, :, 0:PLAIN],
-                    in_=plain_banks[n, tiles.start][:, tiles].rearrange("p t (h f) -> p t h f", f=PLAIN),
-                )
+        def second_product(n, tiles, spare_banks=False):
+            codes, scales = cq_packed[n]
+            if n not in result_tiles:
+                result = results.tile([P, TILES, HEADS, HEAD_DIM], F32, name="result")
+                result_tiles[n] = result
+            plain_bank = psum.tile([P, TILES, HALF], F32, name="x_t" if spare_banks else "plain_bank")
+            rotated_bank = psum.tile([P, TILES, HALF], F32, name="x_t" if spare_banks else "rotated_bank")
+            for t in tiles:
+                for s, bank in enumerate((plain_bank, rotated_bank)):
+                    columns = slice(s * HALF, (s + 1) * HALF)
+                    nc.tensor.matmul_mx(
+                        out=bank[:, t, :],
+                        lhsT=codes[:, t, :].bitcast(FP8X4),
+                        lhsT_scale=scales[:, t, :],
+                        rhs=wb_codes[:, columns].bitcast(FP8X4),
+                        rhs_scale=wb_scales[:, columns],
+                        start=True,
+                        stop=True,
+                    )
+                plain_banks[n, t] = plain_bank
+                rotated_banks[n, t] = rotated_bank
 
-        def rotate_and_store(n):
+        def copy_plain(n, tiles, engine_copy=nc.scalar.copy):
+            part = slice(tiles[0], tiles[-1] + 1)
+            engine_copy(
+                out=result_tiles[n][:, part, :, 0:PLAIN],
+                in_=plain_banks[n, tiles[0]][:, part].rearrange("p t (h f) -> p t h f", f=PLAIN),
+            )
+
+        def rotated_features(n, part):
+            return result_tiles[n][:, part, :, PLAIN:HEAD_DIM].rearrange("p t h (j e) -> p t h j e", e=2)
+
+        def rotate(n, tiles):
+            if n not in from_w_tiles:
+                from_w = stage.tile([P, TILES, HEADS, PAIRS, 2], F32, name="from_w")
+                from_w_tiles[n] = from_w
+            part = slice(tiles[0], tiles[-1] + 1)
             first_table = (n % (TABLES // TILES)) * TILES
-            result = result_tiles[n]
-            from_w = stage.tile([P, TILES, HEADS, PAIRS, 2], F32, name="from_w")
-            rotated_views = []
-            add_engine = nc.gpsimd if n < UNITS - 1 else nc.vector
-            for tiles in steps(n):
-                pairs = rotated_banks[n, tiles.start][:].rearrange("p t (h j e) -> p t h j e", h=HEADS, e=2)
-                shape = [P, tiles.stop - tiles.start, HEADS, PAIRS, 2]
-                tables = slice(first_table + tiles.start, first_table + tiles.stop)
-                rotated = result[:, tiles, :, PLAIN:HEAD_DIM].rearrange("p t h (j e) -> p t h j e", e=2)
-                nc.vector.tensor_tensor(
-                    out=rotated,
-                    in0=pairs[:, tiles, :, :, 0:1].to_broadcast(shape),
-                    in1=cos_sin[:, tables].unsqueeze(2).to_broadcast(shape),
-                    op=ALU.mult,
-                )
-                nc.vector.tensor_tensor(
-                    out=from_w[:, tiles],
-                    in0=pairs[:, tiles, :, :, 1:2].to_broadcast(shape),
-                    in1=nsin_cos[:, tables].unsqueeze(2).to_broadcast(shape),
-                    op=ALU.mult,
-                )
-                rotated_views.append(rotated)
-            for tiles, rotated in zip(steps(n), rotated_views):
-                add_engine.tensor_tensor(out=rotated, in0=rotated, in1=from_w[:, tiles], op=ALU.add)
-                nc.sync.dma_start(out=out_units[n][:, tiles], in_=result[:, tiles].rearrange("p t h d -> p t (h d)"))
+            tables = slice(first_table + part.start, first_table + part.stop)
+            pairs = rotated_banks[n, tiles[0]][:, part].rearrange("p t (h j e) -> p t h j e", h=HEADS, e=2)
+            shape = [P, len(tiles), HEADS, PAIRS, 2]
+            nc.vector.tensor_tensor(
+                out=rotated_features(n, part),
+                in0=pairs[:, :, :, :, 0:1].to_broadcast(shape),
+                in1=cos_sin[:, tables].unsqueeze(2).to_broadcast(shape),
+                op=ALU.mult,
+            )
+            nc.vector.tensor_tensor(
+                out=from_w_tiles[n][:, part],
+                in0=pairs[:, :, :, :, 1:2].to_broadcast(shape),
+                in1=nsin_cos[:, tables].unsqueeze(2).to_broadcast(shape),
+                op=ALU.mult,
+            )
+
+        def add_and_store(n, tiles, engine):
+            part = slice(tiles[0], tiles[-1] + 1)
+            rotated = rotated_features(n, part)
+            engine.tensor_tensor(out=rotated, in0=rotated, in1=from_w_tiles[n][:, part], op=ALU.add)
+            nc.sync.dma_start(
+                out=out_units[n][:, part], in_=result_tiles[n][:, part].rearrange("p t h d -> p t (h d)")
+            )
 
         def vector_copies_plain(n):
-            return False
+            return n % 2 == 1 and n + ROUND_ROTATE < UNITS
 
         def in_range(n):
-            return 0 <= n < UNITS
+            return 0 <= n < UNITS - 2
 
-        for i in range(UNITS + ROUND_ROTATE):
-            if in_range(i):
+        both = [0, 1]
+        for i in range(UNITS + 3):
+            first, second, third = i - ROUND_FIRST, i - ROUND_SECOND, i - ROUND_ROTATE
+            if in_range(first) or first == UNITS - 2:
+                first_product(first, both)
+            if in_range(second):
+                second_product(second, both)
+                if not vector_copies_plain(second):
+                    copy_plain(second, both)
+            if i < UNITS:
                 transpose_x(i)
-            if in_range(i - ROUND_FIRST):
-                first_product(i - ROUND_FIRST)
-            if in_range(i - ROUND_SECOND):
-                second_product(i - ROUND_SECOND)
-                if not vector_copies_plain(i - ROUND_SECOND):
-                    copy_plain(i - ROUND_SECOND, nc.scalar.copy)
-            if in_range(i - ROUND_ROTATE):
-                if vector_copies_plain(i - ROUND_ROTATE):
-                    copy_plain(i - ROUND_ROTATE, nc.vector.tensor_copy)
-                rotate_and_store(i - ROUND_ROTATE)
-            if in_range(i):
-                quantise_x(i)
-            if in_range(i - ROUND_FIRST):
-                quantise_cq(i - ROUND_FIRST)
+            if in_range(third):
+                if vector_copies_plain(third):
+                    copy_plain(third, both, nc.vector.tensor_copy)
+                rotate(third, both)
+                add_and_store(third, both, nc.gpsimd)
+            if i > ROUND_SETUP_A and i + SPLIT_AHEAD < UNITS:
+                split_x(i + SPLIT_AHEAD)
+            if in_range(first):
+                quantise_cq(first, both)
+            if first == UNITS - 2:
+                for t in both:
+                    quantise_cq(first, [t])
             if i == ROUND_SETUP_A:
                 setup_a()
+            if i < UNITS:
+                quantise_x(i)
             if i == ROUND_SETUP_B:
                 setup_b()
-            if i >= ROUND_SETUP_B and in_range(i + 2):
-                split_x(i + 2)
+
+        before, last = UNITS - 2, UNITS - 1
+        rotate(before - 1, both)
+        add_and_store(before - 1, both, nc.gpsimd)
+        for t in both:
+            first_product(last, [t])
+            second_product(before, [t])
+            copy_plain(before, [t])
+        quantise_cq(last, [0])
+        rotate(before, [0])
+        add_and_store(before, [0], nc.gpsimd)
+        quantise_cq(last, [1])
+        for t in both:
+            second_product(last, [t], spare_banks=(t == 0))
+            copy_plain(last, [t])
+        rotate(before, [1])
+        add_and_store(before, [1], nc.gpsimd)
+        rotate(last, [0])
+        rotate(last, [1])
+        add_and_store(last, [0], nc.gpsimd)
+        add_and_store(last, [1], nc.vector)

@@ -39,12 +39,16 @@ FLOPS = 2 * TOKENS * D * QL + 2 * TOKENS * QL * HEADS * HEAD_DIM
 
 TWO_PI = 2.0 * math.pi
 
+ROUND_QUANTISE = 1
 ROUND_FIRST = 4
 ROUND_SECOND = 5
 ROUND_ROTATE = 6
-ROUND_SETUP_A = 1
+ROUND_SETUP_A = 2
 ROUND_SETUP_B = 3
-SPLIT_AHEAD = 3
+LOAD_WQA_AFTER = 1
+LOAD_WQB_AFTER = 3
+BANKS = {"x_t": 3, "cq_t": 2, "plain_bank": 1, "rotated_bank": 2}
+SPLIT_AHEAD = 2
 
 WQA_VECTOR_COLUMNS = 96
 
@@ -85,8 +89,11 @@ def tile_multilatentattention_pa_t_kernel(tc, x, Wqa, Wqb, out):
         x_splits_pool = ctx.enter_context(tc.tile_pool(name="x_splits_pool", bufs=8))
         stage = ctx.enter_context(tc.tile_pool(name="stage", bufs=3))
         results = ctx.enter_context(tc.tile_pool(name="results", bufs=4))
-        psum = ctx.enter_context(tc.psum_pool(name="psum", bufs=2))
+        psum = ctx.enter_context(tc.psum_pool(name="psum", bufs=1))
         ctx.enter_context(tc.manual_schedule())
+
+        def bank(name, shape):
+            return psum.tile(shape, F32, name=name, bufs=BANKS[name])
 
         wa_raw = keep.tile([P, PASSES, PACK, QL], BF16)
         wb_raw = keep.tile([P, PACK, HEADS * HEAD_DIM], BF16)
@@ -100,11 +107,11 @@ def tile_multilatentattention_pa_t_kernel(tc, x, Wqa, Wqb, out):
             else:
                 nc.sync.dma_start(out=x_sb[:], in_=x_units[n])
             x_tiles.append(x_sb)
-            if n == ROUND_SETUP_A:
+            if n == LOAD_WQA_AFTER:
                 wa_passes = Wqa.rearrange("(g p t) c -> g p (t c)", p=P, t=PACK)
                 for g in range(PASSES):
                     nc.sync.dma_start(out=wa_raw[:, g].rearrange("p t c -> p (t c)"), in_=wa_passes[g])
-            if n == ROUND_SETUP_B:
+            if n == LOAD_WQB_AFTER:
                 nc.sync.dma_start(
                     out=wb_raw[:].rearrange("p j f -> p (j f)"), in_=Wqb.rearrange("(p j) f -> p (j f)", j=PACK)
                 )
@@ -163,7 +170,7 @@ def tile_multilatentattention_pa_t_kernel(tc, x, Wqa, Wqb, out):
 
         def split_x(n):
             split = x_splits_pool.tile([P, TILES * D], BF16, align_bytes=64, name="x_split")
-            nc.gpsimd.tensor_copy(
+            nc.vector.tensor_copy(
                 out=split[:].bitcast(F32).rearrange("p (a u i) -> p a u i", u=2, i=P),
                 in_=x_tiles[n][:].bitcast(F32).rearrange("p (a i u) -> p a u i", u=2, i=P),
             )
@@ -180,7 +187,7 @@ def tile_multilatentattention_pa_t_kernel(tc, x, Wqa, Wqb, out):
             grouped = x_stage.tile([P, PASSES * TILES * P * PACK], BF16, align_bytes=64, name="x_grouped")
             grouped_words = grouped[:].bitcast(F32).rearrange("p (g t r u) -> p g t r u", g=PASSES, t=TILES, u=2)
             for t in range(TILES):
-                x_t = psum.tile([P, 2 * PASSES, P], F32, name="x_t")
+                x_t = bank("x_t", [P, 2 * PASSES, P])
                 for g in range(PASSES):
                     first_word = t * WORDS + g * 2 * P
                     for u in range(2):
@@ -204,7 +211,7 @@ def tile_multilatentattention_pa_t_kernel(tc, x, Wqa, Wqb, out):
                 cq_grouped[n] = grouped
             codes, scales = x_packed[n]
             for t in tiles:
-                cq_t = psum.tile([P, PACK, P], F32, name="cq_t")
+                cq_t = bank("cq_t", [P, PACK, P])
                 for m in range(PACK):
                     columns = slice(m * P, (m + 1) * P)
                     for g in range(PASSES):
@@ -232,18 +239,18 @@ def tile_multilatentattention_pa_t_kernel(tc, x, Wqa, Wqb, out):
                 in_=cq_grouped[n][:, part].rearrange("p t r m -> p (t r m)"),
             )
 
-        def second_product(n, tiles, spare_banks=False):
+        def second_product(n, tiles, plain_name="plain_bank", rotated_name="rotated_bank"):
             codes, scales = cq_packed[n]
             if n not in result_tiles:
                 result = results.tile([P, TILES, HEADS, HEAD_DIM], F32, name="result")
                 result_tiles[n] = result
-            plain_bank = psum.tile([P, TILES, HALF], F32, name="x_t" if spare_banks else "plain_bank")
-            rotated_bank = psum.tile([P, TILES, HALF], F32, name="x_t" if spare_banks else "rotated_bank")
+            plain_bank = bank(plain_name, [P, TILES, HALF])
+            rotated_bank = bank(rotated_name, [P, TILES, HALF])
             for t in tiles:
-                for s, bank in enumerate((plain_bank, rotated_bank)):
+                for s, product in enumerate((plain_bank, rotated_bank)):
                     columns = slice(s * HALF, (s + 1) * HALF)
                     nc.tensor.matmul_mx(
-                        out=bank[:, t, :],
+                        out=product[:, t, :],
                         lhsT=codes[:, t, :].bitcast(FP8X4),
                         lhsT_scale=scales[:, t, :],
                         rhs=wb_codes[:, columns].bitcast(FP8X4),
@@ -294,59 +301,60 @@ def tile_multilatentattention_pa_t_kernel(tc, x, Wqa, Wqb, out):
                 out=out_units[n][:, part], in_=result_tiles[n][:, part].rearrange("p t h d -> p t (h d)")
             )
 
-        def vector_copies_plain(n):
-            return n % 2 == 1 and n + ROUND_ROTATE < UNITS
+        def splits(n):
+            return n > ROUND_FIRST
 
         def in_range(n):
-            return 0 <= n < UNITS - 2
+            return 0 <= n < UNITS
 
         both = [0, 1]
-        for i in range(UNITS + 3):
-            first, second, third = i - ROUND_FIRST, i - ROUND_SECOND, i - ROUND_ROTATE
-            if in_range(first) or first == UNITS - 2:
+        for i in range(UNITS + ROUND_FIRST - 1):
+            quantise, first, second, third = (
+                i - ROUND_QUANTISE,
+                i - ROUND_FIRST,
+                i - ROUND_SECOND,
+                i - ROUND_ROTATE,
+            )
+            if in_range(first):
                 first_product(first, both)
             if in_range(second):
                 second_product(second, both)
-                if not vector_copies_plain(second):
-                    copy_plain(second, both)
-            if i < UNITS:
-                transpose_x(i)
+                copy_plain(second, both)
             if in_range(third):
-                if vector_copies_plain(third):
-                    copy_plain(third, both, nc.vector.tensor_copy)
                 rotate(third, both)
                 add_and_store(third, both, nc.gpsimd)
-            if i > ROUND_SETUP_A and i + SPLIT_AHEAD < UNITS:
-                split_x(i + SPLIT_AHEAD)
             if in_range(first):
                 quantise_cq(first, both)
-            if first == UNITS - 2:
-                for t in both:
-                    quantise_cq(first, [t])
             if i == ROUND_SETUP_A:
                 setup_a()
-            if i < UNITS:
-                quantise_x(i)
+            if in_range(quantise):
+                quantise_x(quantise)
             if i == ROUND_SETUP_B:
                 setup_b()
+            if i + SPLIT_AHEAD < UNITS and splits(i + SPLIT_AHEAD):
+                split_x(i + SPLIT_AHEAD)
+            if in_range(i):
+                transpose_x(i)
 
         before, last = UNITS - 2, UNITS - 1
         rotate(before - 1, both)
         add_and_store(before - 1, both, nc.gpsimd)
         for t in both:
             first_product(last, [t])
-            second_product(before, [t])
-            copy_plain(before, [t])
-        quantise_cq(last, [0])
-        rotate(before, [0])
-        add_and_store(before, [0], nc.gpsimd)
-        quantise_cq(last, [1])
+        second_product(before, [0])
+        copy_plain(before, [0])
+        second_product(before, [1], "x_t", "x_t")
+        copy_plain(before, [1])
         for t in both:
-            second_product(last, [t], spare_banks=(t == 0))
-            copy_plain(last, [t])
-        rotate(before, [1])
-        add_and_store(before, [1], nc.gpsimd)
-        rotate(last, [0])
-        rotate(last, [1])
+            quantise_cq(last, [t])
+        second_product(last, [0], "x_t", "rotated_bank")
+        copy_plain(last, [0])
+        second_product(last, [1], "cq_t", "cq_t")
+        copy_plain(last, [1])
+        for t in both:
+            rotate(before, [t])
+            add_and_store(before, [t], nc.gpsimd)
+        for t in both:
+            rotate(last, [t])
         add_and_store(last, [0], nc.gpsimd)
         add_and_store(last, [1], nc.vector)

@@ -86,9 +86,9 @@ def tile_multilatentattention_pa_t_kernel(tc, x, Wqa, Wqb, out):
         keep = ctx.enter_context(tc.tile_pool(name="keep", bufs=1))
         x_pool = ctx.enter_context(tc.tile_pool(name="x_pool", bufs=UNITS))
         x_stage = ctx.enter_context(tc.tile_pool(name="x_stage", bufs=ROUND_FIRST + 2))
-        x_splits_pool = ctx.enter_context(tc.tile_pool(name="x_splits_pool", bufs=8))
+        x_splits_pool = ctx.enter_context(tc.tile_pool(name="x_splits_pool", bufs=4))
         stage = ctx.enter_context(tc.tile_pool(name="stage", bufs=3))
-        results = ctx.enter_context(tc.tile_pool(name="results", bufs=4))
+        results = ctx.enter_context(tc.tile_pool(name="results", bufs=8))
         psum = ctx.enter_context(tc.psum_pool(name="psum", bufs=1))
         ctx.enter_context(tc.manual_schedule())
 
@@ -322,7 +322,8 @@ def tile_multilatentattention_pa_t_kernel(tc, x, Wqa, Wqb, out):
                 copy_plain(second, both)
             if in_range(third):
                 rotate(third, both)
-                add_and_store(third, both, nc.gpsimd)
+                for tiles in [both] if third < UNITS - ROUND_FIRST else [[0], [1]]:
+                    add_and_store(third, tiles, nc.gpsimd)
             if in_range(first):
                 quantise_cq(first, both)
             if i == ROUND_SETUP_A:
@@ -338,23 +339,25 @@ def tile_multilatentattention_pa_t_kernel(tc, x, Wqa, Wqb, out):
 
         before, last = UNITS - 2, UNITS - 1
         rotate(before - 1, both)
-        add_and_store(before - 1, both, nc.gpsimd)
         for t in both:
-            first_product(last, [t])
+            add_and_store(before - 1, [t], nc.gpsimd)
+        first_product(last, [0])
         second_product(before, [0])
         copy_plain(before, [0])
+        first_product(last, [1])
         second_product(before, [1], "x_t", "x_t")
         copy_plain(before, [1])
-        for t in both:
-            quantise_cq(last, [t])
+        quantise_cq(last, [0])
+        rotate(before, [0])
+        add_and_store(before, [0], nc.gpsimd)
+        quantise_cq(last, [1])
         second_product(last, [0], "x_t", "rotated_bank")
         copy_plain(last, [0])
         second_product(last, [1], "cq_t", "cq_t")
         copy_plain(last, [1])
-        for t in both:
-            rotate(before, [t])
-            add_and_store(before, [t], nc.gpsimd)
-        for t in both:
-            rotate(last, [t])
+        rotate(before, [1])
+        add_and_store(before, [1], nc.gpsimd)
+        rotate(last, [0])
         add_and_store(last, [0], nc.gpsimd)
+        rotate(last, [1])
         add_and_store(last, [1], nc.vector)

@@ -282,14 +282,14 @@ def tile_multilatentattention_pa_t_kernel(tc, x, Wqa, Wqb, out):
             shape = [P, len(tiles), HEADS, PAIRS, 2]
             nc.vector.tensor_tensor(
                 out=rotated_features(n, part),
-                in0=pairs[:, :, :, :, 0:1].to_broadcast(shape),
-                in1=cos_sin[:, tables].unsqueeze(2).to_broadcast(shape),
+                in0=cos_sin[:, tables].unsqueeze(2).to_broadcast(shape),
+                in1=pairs[:, :, :, :, 0:1].to_broadcast(shape),
                 op=ALU.mult,
             )
             nc.vector.tensor_tensor(
                 out=from_w_tiles[n][:, part],
-                in0=pairs[:, :, :, :, 1:2].to_broadcast(shape),
-                in1=nsin_cos[:, tables].unsqueeze(2).to_broadcast(shape),
+                in0=nsin_cos[:, tables].unsqueeze(2).to_broadcast(shape),
+                in1=pairs[:, :, :, :, 1:2].to_broadcast(shape),
                 op=ALU.mult,
             )
 

import math
from contextlib import ExitStack

import concourse.masks as masks
import concourse.mybir as mybir

F32 = mybir.dt.float32
BF16 = mybir.dt.bfloat16
I32 = mybir.dt.int32
U32 = mybir.dt.uint32
U8 = mybir.dt.uint8
FP8X4 = mybir.dt.float8_e4m3fn_x4
ALU = mybir.AluOpType
SIN = mybir.ActivationFunctionType.Sin

P = 128
PACK = 4
K_PASS = P * PACK

TOKENS = 4 * 1024
SEQ = 1024
D = 1024
QL = 512
HEADS = 4
HEAD_DIM = 128
PLAIN = 64
PAIRS = 32
BASE = 10000.0

PASSES = D // K_PASS
WORDS = D // 2
TILES = 2
UNIT = TILES * P
UNITS = TOKENS // UNIT
TABLES = SEQ // P
HALF = HEADS * PLAIN

FLOPS = 2 * TOKENS * D * QL + 2 * TOKENS * QL * HEADS * HEAD_DIM

TWO_PI = 2.0 * math.pi

ROUND_QUANTISE = 1
ROUND_FIRST = 4
ROUND_SECOND = 5
ROUND_ROTATE = 6
ROUND_SETUP_A = 2
ROUND_SETUP_B = 3
LOAD_WQA_AFTER = 1
LOAD_WQB_AFTER = 3
BANKS = {"x_t": 3, "cq_t": 2, "plain_bank": 1, "rotated_bank": 2}
SPLIT_AHEAD = 2

WQA_VECTOR_COLUMNS = 96


def rotation_phases(nc, pool, position_int):
    shape = [P, TABLES, PAIRS, 2]
    turns = pool.tile(shape, F32)
    nc.vector.tensor_scalar(
        out=turns[:, :, 0:1, 1], in0=position_int[:].unsqueeze(2), scalar1=1.0 / TWO_PI, scalar2=None, op0=ALU.mult
    )
    for n in (1, 2, 4, 8, 16):
        nc.vector.tensor_scalar(
            out=turns[:, :, n : 2 * n, 1],
            in0=turns[:, :, 0:n, 1],
            scalar1=BASE ** (-n / PAIRS),
            scalar2=None,
            op0=ALU.mult,
        )
    nc.vector.tensor_scalar(out=turns[:, :, :, 0], in0=turns[:, :, :, 1], scalar1=0.25, scalar2=None, op0=ALU.add)
    whole_int = pool.tile(shape, I32)
    nc.vector.tensor_copy(out=whole_int[:], in_=turns[:])
    whole = pool.tile(shape, F32)
    nc.vector.tensor_copy(out=whole[:], in_=whole_int[:])
    phase = pool.tile(shape, F32)
    nc.vector.tensor_tensor(out=phase[:], in0=turns[:], in1=whole[:], op=ALU.subtract)
    return phase


def tile_multilatentattention_pa_t_kernel(tc, x, Wqa, Wqb, out):
    nc = tc.nc
    x_units = x.flatten_outer_dims().rearrange("(n p t) k -> n p (t k)", p=P, t=TILES)
    out_units = out.rearrange("b s h d -> (b s) (h d)").rearrange("(n p t) f -> n p t f", p=P, t=TILES)

    with ExitStack() as ctx:
        keep = ctx.enter_context(tc.tile_pool(name="keep", bufs=1))
        x_pool = ctx.enter_context(tc.tile_pool(name="x_pool", bufs=UNITS))
        x_stage = ctx.enter_context(tc.tile_pool(name="x_stage", bufs=ROUND_FIRST + 2))
        x_splits_pool = ctx.enter_context(tc.tile_pool(name="x_splits_pool", bufs=4))
        stage = ctx.enter_context(tc.tile_pool(name="stage", bufs=3))
        results = ctx.enter_context(tc.tile_pool(name="results", bufs=8))
        psum = ctx.enter_context(tc.psum_pool(name="psum", bufs=1))
        ctx.enter_context(tc.manual_schedule())

        def bank(name, shape):
            return psum.tile(shape, F32, name=name, bufs=BANKS[name])

        wa_raw = keep.tile([P, PASSES, PACK, QL], BF16)
        wb_raw = keep.tile([P, PACK, HEADS * HEAD_DIM], BF16)
        x_tiles = []
        for n in range(UNITS):
            x_sb = x_pool.tile([P, TILES * D], BF16)
            if n == 0:
                for t in range(TILES):
                    columns = slice(t * D, (t + 1) * D)
                    nc.sync.dma_start(out=x_sb[:, columns], in_=x_units[n][:, columns])
            else:
                nc.sync.dma_start(out=x_sb[:], in_=x_units[n])
            x_tiles.append(x_sb)
            if n == LOAD_WQA_AFTER:
                wa_passes = Wqa.rearrange("(g p t) c -> g p (t c)", p=P, t=PACK)
                for g in range(PASSES):
                    nc.sync.dma_start(out=wa_raw[:, g].rearrange("p t c -> p (t c)"), in_=wa_passes[g])
            if n == LOAD_WQB_AFTER:
                nc.sync.dma_start(
                    out=wb_raw[:].rearrange("p j f -> p (j f)"), in_=Wqb.rearrange("(p j) f -> p (j f)", j=PACK)
                )

        identity = keep.tile([P, P], F32)
        masks.make_identity(nc, identity[:])
        position_int = keep.tile([P, TABLES], I32)
        nc.gpsimd.iota(
            position_int[:], pattern=[[UNIT, TABLES // TILES], [1, TILES]], base=0, channel_multiplier=TILES
        )
        phase = rotation_phases(nc, keep, position_int)
        first_sine = keep.tile([P, 1], F32)
        nc.scalar.activation(out=first_sine[:], in_=identity[:, 0:1], func=SIN)
        cos_sin = keep.tile([P, TABLES, PAIRS, 2], F32)
        nsin_cos = keep.tile([P, TABLES, PAIRS, 2], F32)
        wa_codes = keep.tile([P, PASSES, QL], U32, align_bytes=64)
        wa_scales = keep.tile([P, PASSES, QL], U8, align_bytes=64)
        wb_codes = keep.tile([P, 2 * HALF], U32, align_bytes=64)
        wb_scales = keep.tile([P, 2 * HALF], U8, align_bytes=64)

        def setup_a():
            nc.scalar.activation(out=cos_sin[:], in_=phase[:], func=SIN, scale=TWO_PI)
            for e, sign in enumerate((-1.0, 1.0)):
                nc.gpsimd.tensor_scalar(
                    out=nsin_cos[:, :, :, e],
                    in0=cos_sin[:, :, :, 1 - e],
                    scalar1=sign,
                    scalar2=0.0,
                    op0=ALU.mult,
                    op1=ALU.add,
                )
            wa_grouped = keep.tile([P, PASSES, QL * PACK], BF16, align_bytes=64)
            for g in range(PASSES):
                wa_sorted = wa_grouped[:, g].rearrange("p (m i t) -> p m i t", m=PACK, t=PACK)
                wa_rows = wa_raw[:, g].rearrange("p t (i m) -> p m i t", m=PACK)
                nc.vector.tensor_copy(
                    out=wa_sorted[:, :, 0:WQA_VECTOR_COLUMNS], in_=wa_rows[:, :, 0:WQA_VECTOR_COLUMNS]
                )
                nc.scalar.copy(out=wa_sorted[:, :, WQA_VECTOR_COLUMNS:P], in_=wa_rows[:, :, WQA_VECTOR_COLUMNS:P])
            for g in range(PASSES):
                nc.vector.quantize_mx(out=wa_codes[:, g].bitcast(FP8X4), scales=wa_scales[:, g], in_=wa_grouped[:, g])

        def setup_b():
            wb_grouped = keep.tile([P, 2, HALF * PACK], BF16, align_bytes=64)
            wb_sorted = wb_raw[:].rearrange("p j (h s f) -> p s h f j", s=2, f=PLAIN)
            for s in range(2):
                nc.vector.tensor_copy(
                    out=wb_grouped[:, s].rearrange("p (h f j) -> p h f j", h=HEADS, j=PACK), in_=wb_sorted[:, s]
                )
            nc.vector.quantize_mx(
                out=wb_codes[:].bitcast(FP8X4), scales=wb_scales[:], in_=wb_grouped[:].rearrange("p s c -> p (s c)")
            )

        x_splits, x_packed, cq_grouped, cq_packed = {}, {}, {}, {}
        plain_banks, rotated_banks, result_tiles, from_w_tiles = {}, {}, {}, {}

        def split_x(n):
            split = x_splits_pool.tile([P, TILES * D], BF16, align_bytes=64, name="x_split")
            nc.vector.tensor_copy(
                out=split[:].bitcast(F32).rearrange("p (a u i) -> p a u i", u=2, i=P),
                in_=x_tiles[n][:].bitcast(F32).rearrange("p (a i u) -> p a u i", u=2, i=P),
            )
            x_splits[n] = split

        def word_columns(n, first_word, u):
            if n in x_splits:
                return x_splits[n][:].bitcast(F32)[:, first_word + u * P : first_word + (u + 1) * P]
            return x_tiles[n][:].bitcast(F32)[:, first_word + u : first_word + 2 * P : 2]

        x_grouped = {}

        def transpose_x(n):
            grouped = x_stage.tile([P, PASSES * TILES * P * PACK], BF16, align_bytes=64, name="x_grouped")
            grouped_words = grouped[:].bitcast(F32).rearrange("p (g t r u) -> p g t r u", g=PASSES, t=TILES, u=2)
            for t in range(TILES):
                x_t = bank("x_t", [P, 2 * PASSES, P])
                for g in range(PASSES):
                    first_word = t * WORDS + g * 2 * P
                    for u in range(2):
                        nc.tensor.transpose(x_t[:, 2 * g + u, :], word_columns(n, first_word, u), identity[:])
                nc.scalar.copy(out=grouped_words[:, :, t], in_=x_t[:].rearrange("p (g u) r -> p g r u", u=2))
            x_grouped[n] = grouped

        def quantise_x(n):
            codes = x_stage.tile([P, PASSES, TILES, P], U32, align_bytes=64, name="x_codes")
            scales = x_stage.tile([P, PASSES, TILES, P], U8, align_bytes=64, name="x_scales")
            nc.vector.quantize_mx(
                out=codes[:].rearrange("p g t r -> p (g t r)").bitcast(FP8X4),
                scales=scales[:].rearrange("p g t r -> p (g t r)"),
                in_=x_grouped[n][:],
            )
            x_packed[n] = (codes, scales)

        def first_product(n, tiles):
            if n not in cq_grouped:
                grouped = stage.tile([P, TILES, P, PACK], BF16, align_bytes=64, name="cq_grouped")
                cq_grouped[n] = grouped
            codes, scales = x_packed[n]
            for t in tiles:
                cq_t = bank("cq_t", [P, PACK, P])
                for m in range(PACK):
                    columns = slice(m * P, (m + 1) * P)
                    for g in range(PASSES):
                        nc.tensor.matmul_mx(
                            out=cq_t[:, m, :],
                            lhsT=wa_codes[:, g, columns].bitcast(FP8X4),
                            lhsT_scale=wa_scales[:, g, columns],
                            rhs=codes[:, g, t, :].bitcast(FP8X4),
                            rhs_scale=scales[:, g, t, :],
                            start=(g == 0),
                            stop=(g == PASSES - 1),
                        )
                nc.scalar.copy(out=cq_grouped[n][:, t], in_=cq_t[:].rearrange("p m r -> p r m"))

        def quantise_cq(n, tiles):
            if n not in cq_packed:
                codes = stage.tile([P, TILES, P], U32, align_bytes=64, name="cq_codes")
                scales = stage.tile([P, TILES, P], U8, align_bytes=64, name="cq_scales")
                cq_packed[n] = (codes, scales)
            codes, scales = cq_packed[n]
            part = slice(tiles[0], tiles[-1] + 1)
            nc.vector.quantize_mx(
                out=codes[:, part].rearrange("p t r -> p (t r)").bitcast(FP8X4),
                scales=scales[:, part].rearrange("p t r -> p (t r)"),
                in_=cq_grouped[n][:, part].rearrange("p t r m -> p (t r m)"),
            )

        def second_product(n, tiles, plain_name="plain_bank", rotated_name="rotated_bank"):
            codes, scales = cq_packed[n]
            if n not in result_tiles:
                result = results.tile([P, TILES, HEADS, HEAD_DIM], F32, name="result")
                result_tiles[n] = result
            plain_bank = bank(plain_name, [P, TILES, HALF])
            rotated_bank = bank(rotated_name, [P, TILES, HALF])
            for t in tiles:
                for s, product in enumerate((plain_bank, rotated_bank)):
                    columns = slice(s * HALF, (s + 1) * HALF)
                    nc.tensor.matmul_mx(
                        out=product[:, t, :],
                        lhsT=codes[:, t, :].bitcast(FP8X4),
                        lhsT_scale=scales[:, t, :],
                        rhs=wb_codes[:, columns].bitcast(FP8X4),
                        rhs_scale=wb_scales[:, columns],
                        start=True,
                        stop=True,
                    )
                plain_banks[n, t] = plain_bank
                rotated_banks[n, t] = rotated_bank

        def copy_plain(n, tiles, engine_copy=nc.scalar.copy):
            part = slice(tiles[0], tiles[-1] + 1)
            engine_copy(
                out=result_tiles[n][:, part, :, 0:PLAIN],
                in_=plain_banks[n, tiles[0]][:, part].rearrange("p t (h f) -> p t h f", f=PLAIN),
            )

        def rotated_features(n, part):
            return result_tiles[n][:, part, :, PLAIN:HEAD_DIM].rearrange("p t h (j e) -> p t h j e", e=2)

        def rotate(n, tiles):
            if n not in from_w_tiles:
                from_w = stage.tile([P, TILES, HEADS, PAIRS, 2], F32, name="from_w")
                from_w_tiles[n] = from_w
            part = slice(tiles[0], tiles[-1] + 1)
            first_table = (n % (TABLES // TILES)) * TILES
            tables = slice(first_table + part.start, first_table + part.stop)
            pairs = rotated_banks[n, tiles[0]][:, part].rearrange("p t (h j e) -> p t h j e", h=HEADS, e=2)
            shape = [P, len(tiles), HEADS, PAIRS, 2]
            nc.vector.tensor_tensor(
                out=rotated_features(n, part),
                in0=cos_sin[:, tables].unsqueeze(2).to_broadcast(shape),
                in1=pairs[:, :, :, :, 0:1].to_broadcast(shape),
                op=ALU.mult,
            )
            nc.vector.tensor_tensor(
                out=from_w_tiles[n][:, part],
                in0=nsin_cos[:, tables].unsqueeze(2).to_broadcast(shape),
                in1=pairs[:, :, :, :, 1:2].to_broadcast(shape),
                op=ALU.mult,
            )

        def add_and_store(n, tiles, engine):
            part = slice(tiles[0], tiles[-1] + 1)
            rotated = rotated_features(n, part)
            engine.tensor_tensor(out=rotated, in0=rotated, in1=from_w_tiles[n][:, part], op=ALU.add)
            nc.sync.dma_start(
                out=out_units[n][:, part], in_=result_tiles[n][:, part].rearrange("p t h d -> p t (h d)")
            )

        def splits(n):
            return n > ROUND_FIRST

        def in_range(n):
            return 0 <= n < UNITS

        both = [0, 1]
        for i in range(UNITS + ROUND_FIRST - 1):
            quantise, first, second, third = (
                i - ROUND_QUANTISE,
                i - ROUND_FIRST,
                i - ROUND_SECOND,
                i - ROUND_ROTATE,
            )
            if in_range(first):
                first_product(first, both)
            if in_range(second):
                second_product(second, both)
                copy_plain(second, both)
            if in_range(third):
                rotate(third, both)
                for tiles in [both] if third < UNITS - ROUND_FIRST else [[0], [1]]:
                    add_and_store(third, tiles, nc.gpsimd)
            if in_range(first):
                quantise_cq(first, both)
            if i == ROUND_SETUP_A:
                setup_a()
            if in_range(quantise):
                quantise_x(quantise)
            if i == ROUND_SETUP_B:
                setup_b()
            if i + SPLIT_AHEAD < UNITS and splits(i + SPLIT_AHEAD):
                split_x(i + SPLIT_AHEAD)
            if in_range(i):
                transpose_x(i)

        before, last = UNITS - 2, UNITS - 1
        rotate(before - 1, both)
        for t in both:
            add_and_store(before - 1, [t], nc.gpsimd)
        first_product(last, [0])
        second_product(before, [0])
        copy_plain(before, [0])
        first_product(last, [1])
        second_product(before, [1], "x_t", "x_t")
        copy_plain(before, [1])
        quantise_cq(last, [0])
        rotate(before, [0])
        add_and_store(before, [0], nc.gpsimd)
        quantise_cq(last, [1])
        second_product(last, [0], "x_t", "rotated_bank")
        copy_plain(last, [0])
        second_product(last, [1], "cq_t", "cq_t")
        copy_plain(last, [1])
        rotate(before, [1])
        add_and_store(before, [1], nc.gpsimd)
        rotate(last, [0])
        add_and_store(last, [0], nc.gpsimd)
        rotate(last, [1])
        add_and_store(last, [1], nc.vector)
